import numpy as np
import ml_dtypes


def mxq(x, axis, fmt="e4m3"):
    dtype, down = {"e4m3": (ml_dtypes.float8_e4m3fn, 7), "e5m2": (ml_dtypes.float8_e5m2, 14)}[fmt]
    v = np.moveaxis(np.asarray(x, np.float32).astype(ml_dtypes.bfloat16).astype(np.float64), axis, -1)
    blocks = v.reshape(v.shape[:-1] + (-1, 32))
    amax = np.abs(blocks).max(-1, keepdims=True)
    byte = np.maximum(np.where(amax > 0, np.frexp(amax)[1] - 1 + 127, 0) - down, 1)
    scale = np.exp2(byte - 127.0)
    codes = (blocks / scale).astype(np.float32).astype(dtype).astype(np.float64)
    return np.moveaxis((codes * scale).reshape(v.shape), -1, axis)


WIDE = False


def mx_kscale(k):
    if not WIDE:
        return np.ones(k)
    levels = np.array([10, -10, 5, -5, 0])
    if k % 512:
        return np.exp2(np.random.permutation(np.resize(levels, k // 32))).repeat(32)
    a = np.empty((k // 512, 16))
    for p in range(k // 512):
        a[p, :8] = np.random.permutation(np.resize(levels, 8))
        for g in range(8):
            far = levels[np.abs(levels - a[p, g]) >= 10]
            a[p, g + 8] = far[np.random.randint(len(far))]
    return np.exp2(a.ravel()).repeat(32)


BF16 = ml_dtypes.bfloat16


def bf(x):
    return np.asarray(x, np.float32).astype(BF16)


def f64(x):
    return np.asarray(x).astype(np.float64)


E2M1 = np.array([0.0, 0.5, 1.0, 1.5, 2.0, 3.0, 4.0, 6.0, -0.0, -0.5, -1.0, -1.5, -2.0, -3.0, -4.0, -6.0])


def pack_weight(w, fmt):
    k, n = w.shape
    w = f64(bf(w)).reshape(k // 32, 32, n)
    amax = np.abs(w).max(1)
    if fmt == "e4m3":
        byte = np.frexp(amax)[1] - 1 + 127 - 7
    else:
        mant, ex = np.frexp(amax / 6.0)
        byte = np.where(mant > 0.5, ex, ex - 1) + 127
    byte = np.clip(np.where(amax > 0, byte, 1), 1, 254)
    scaled = (w * np.exp2(127.0 - byte)[:, None, :]).reshape(k, n).astype(np.float32)
    by_word = np.ascontiguousarray(scaled.reshape(k // 512, 128, 4, n).transpose(0, 1, 3, 2))
    if fmt == "e4m3":
        words = by_word.astype(ml_dtypes.float8_e4m3fn).view(np.uint8)
    else:
        c = by_word.astype(ml_dtypes.float4_e2m1fn).view(np.uint8) & 0xF
        words = c[..., 0::2] | (c[..., 1::2] << 4)
    return np.ascontiguousarray(words), np.ascontiguousarray(byte.astype(np.uint8).reshape(k // 512, 16, n))


def unpack_weight(words, scales, fmt):
    g, p, n, _ = words.shape
    if fmt == "e4m3":
        vals = np.ascontiguousarray(words).view(ml_dtypes.float8_e4m3fn).astype(np.float64)
    else:
        nib = np.empty((g, p, n, 4), np.uint8)
        nib[..., 0::2] = words & 0xF
        nib[..., 1::2] = words >> 4
        vals = E2M1[nib]
    vals = vals * np.repeat(np.exp2(scales.astype(np.float64) - 127.0), 8, axis=1)[..., None]
    return vals.transpose(0, 1, 3, 2).reshape(g * 512, n)
def pack4(w):
    words, scales = pack_weight(w, "e2m1")
    return words.reshape(words.shape[0], 128, -1), scales


def unpack4(words, scales):
    return unpack_weight(words.reshape(words.shape[0], 128, -1, 2), scales, "e2m1")


NB, D, CO, CV, R = 8, 256, 1024, 512, 512


def draw0():
    s, t = mx_kscale(CV), mx_kscale(R)
    x1 = bf(np.random.standard_normal((NB, D, CO)))
    A = bf(np.random.standard_normal((D, R)) / np.sqrt(D) * t)
    t2 = bf(np.random.standard_normal((NB, R, CV)) * s)
    w = bf(np.random.standard_normal((NB, CO, CV)) / np.sqrt(CV) / s)
    words, scales = pack4((np.random.standard_normal((D, R)) / np.sqrt(R) / t).T)
    return {"x1": x1,
            "A": A,
            "t2": t2,
            "w": w,
            "C_words": words,
            "C_scales": scales}


def core(x1, A, t2, w, C_words, C_scales):
    t1 = f64(A).T @ f64(x1)
    t3 = mxq(f64(t2), 2, "e4m3") @ mxq(f64(w).transpose(0, 2, 1), 1, "e4m3")
    h = t1 * t3
    return unpack4(C_words, C_scales).T @ mxq(h, 1, "e4m3")


def e4m3fn_bytes(y):
    return np.clip(np.asarray(y, np.float64), -448.0, 448.0).astype(np.float32).astype(ml_dtypes.float8_e4m3fn).view(np.uint8)


def e4m3fn_values(b):
    return np.asarray(b, np.uint8).view(ml_dtypes.float8_e4m3fn).astype(np.float64)


def setup_inputs():
    d = draw0()
    x0 = np.asarray(d['w']).astype(np.float64)
    s = (np.max(np.abs(x0), axis=(0, 1), keepdims=True) / 448.0).astype(np.float32)
    out = {}
    for k, v in d.items():
        if k == 'w':
            out['w_bytes'] = e4m3fn_bytes(x0 / s.astype(np.float64))
            out['w_scale'] = s
        else:
            out[k] = v
    return out


def reference(x1, A, t2, w_bytes, w_scale, C_words, C_scales):
    return core(x1, A, t2, e4m3fn_values(w_bytes) * w_scale.astype(np.float64), C_words, C_scales)

@@ -1,0 +1,247 @@
+from contextlib import ExitStack
+
+import concourse.mybir as mybir
+from concourse.masks import make_identity
+
+NB, D, CO, CV, R = 8, 256, 1024, 512, 512
+FLOPS = 2 * NB * (R * D * CO + R * CV * CO + D * R * CO)
+
+F32 = mybir.dt.float32
+BF16 = mybir.dt.bfloat16
+I32 = mybir.dt.int32
+U32 = mybir.dt.uint32
+U8 = mybir.dt.uint8
+FP8 = mybir.dt.float8_e4m3fn
+FP8X4 = mybir.dt.float8_e4m3fn_x4
+FP4X4 = mybir.dt.float4_e2m1fn_x4
+MULT = mybir.AluOpType.mult
+
+P = 128
+HALF = 512
+UNITS = NB * CO // HALF
+SLOTS = HALF // P
+AHEAD = 3
+
+
+def tile_cptensorproduct_pa_t_w4_kernel(tc, x1, A, t2, w_bytes, w_scale, C_words, C_scales, out):
+    nc = tc.nc
+    with ExitStack() as ctx:
+        const = ctx.enter_context(tc.tile_pool(name="const", bufs=1))
+        loads = ctx.enter_context(tc.tile_pool(name="loads", bufs=4))
+        work = ctx.enter_context(tc.tile_pool(name="work", bufs=3))
+        psum = ctx.enter_context(tc.psum_pool(name="psum", bufs=2))
+        ctx.enter_context(tc.manual_schedule())
+
+        x1_sb, t2_sb, w_sb = {}, {}, {}
+        w_bf, w_group, w_codes, w_scales = {}, {}, {}, {}
+        t2_group, t2_codes, t2_scales = {}, {}, {}
+        t1_sb, h_bf, h_codes, h_scales, out_sb = {}, {}, {}, {}, {}
+
+        def load_w(i):
+            b, half = divmod(i, 2)
+            t = loads.tile([P, SLOTS, CV], U8, name="w_raw", bufs=8)
+            rows = w_bytes[b, half * HALF : (half + 1) * HALF, :]
+            nc.sync.dma_start(out=t[:], in_=rows.rearrange("(j p) c -> p j c", p=P))
+            w_sb[i] = t
+
+        def load_t2(b):
+            t = loads.tile([P, 4, CV], BF16, name="t2_raw")
+            nc.sync.dma_start(out=t[:], in_=t2[b].rearrange("(m t) c -> m t c", t=4))
+            t2_sb[b] = t
+
+        def load_x1(b):
+            t = loads.tile([P, 2, CO], BF16, name="x1_raw")
+            nc.sync.dma_start(out=t[:], in_=x1[b].rearrange("(p k) o -> p k o", k=2))
+            x1_sb[b] = t
+
+        def load_sample(b):
+            load_w(2 * b)
+            load_t2(b)
+            load_x1(b)
+            load_w(2 * b + 1)
+
+        def scale_w(i, j):
+            if i >= UNITS:
+                return
+            if j == 0:
+                w_bf[i] = work.tile([P, SLOTS, CV], BF16, name="w_wide", align_bytes=64)
+            nc.vector.tensor_tensor(out=w_bf[i][:, j, :], in0=w_sb[i][:, j, :].bitcast(FP8), in1=scale_row[:], op=MULT)
+
+        def turn_pair(src, pair, dst):
+            words = src[:].rearrange("p j c -> p (j c)").bitcast(F32)
+            bank = psum.tile([P, 2, 2, P], F32, name="turned", bufs=3)
+            for jj in range(2):
+                first = 256 * (2 * pair + jj)
+                for u in range(2):
+                    nc.tensor.transpose(bank[:, jj, u, :], words[:, first + u : first + 256 : 2], ident[:])
+            cols = dst[:].bitcast(F32)[:, 512 * pair : 512 * (pair + 1)]
+            nc.scalar.copy(out=cols.rearrange("p (j r u) -> p j r u", j=2, u=2), in_=bank[:].rearrange("p j u r -> p j r u"))
+
+        def turn_w(i):
+            if i >= UNITS:
+                return
+            w_group[i] = work.tile([P, 4 * HALF], BF16, name="w_grouped", align_bytes=64)
+            for pair in range(2):
+                turn_pair(w_bf[i], pair, w_group[i])
+
+        def turn_t2(b, pair):
+            if b >= NB:
+                return
+            if pair == 0:
+                t2_group[b] = work.tile([P, 4 * R], BF16, name="t2_grouped", bufs=2, align_bytes=64)
+            turn_pair(t2_sb[b], pair, t2_group[b])
+
+        def quantise_w(i):
+            if i >= UNITS:
+                return
+            w_codes[i] = work.tile([P, HALF], U32, name="w_code", align_bytes=64)
+            w_scales[i] = work.tile([P, HALF], U8, name="w_scl", align_bytes=64)
+            nc.vector.quantize_mx(out=w_codes[i][:].bitcast(FP8X4), scales=w_scales[i][:], in_=w_group[i][:])
+
+        def quantise_t2(b):
+            if b >= NB:
+                return
+            t2_codes[b] = work.tile([P, R], U32, name="t2_code", bufs=2, align_bytes=64)
+            t2_scales[b] = work.tile([P, R], U8, name="t2_scl", bufs=2, align_bytes=64)
+            nc.vector.quantize_mx(out=t2_codes[b][:].bitcast(FP8X4), scales=t2_scales[b][:], in_=t2_group[b][:])
+
+        def product_t1(s):
+            if s >= UNITS * SLOTS:
+                return
+            b, block = divmod(s, CO // P)
+            bank = psum.tile([P, 4, P], F32, name="t1_bank")
+            for t in range(4):
+                for k in range(2):
+                    nc.tensor.matmul(
+                        bank[:, t, :],
+                        lhsT=a_perm[:, k, t, :],
+                        rhs=x1_sb[b][:, k, P * block : P * (block + 1)],
+                        start=(k == 0),
+                        stop=(k == 1),
+                    )
+            t1_sb[s] = work.tile([P, P, 4], F32, name="t1_copy")
+            nc.scalar.copy(out=t1_sb[s][:], in_=bank[:].rearrange("p t o -> p o t"))
+
+        def product_t3(s):
+            i, j = divmod(s, SLOTS)
+            b = i // 2
+            bank = psum.tile([P, 4, P], F32, name="t3_bank")
+            for t in range(4):
+                m = slice(P * t, P * (t + 1))
+                n = slice(P * j, P * (j + 1))
+                nc.tensor.matmul_mx(
+                    out=bank[:, t, :],
+                    lhsT=t2_codes[b][:, m].bitcast(FP8X4),
+                    lhsT_scale=t2_scales[b][:, m],
+                    rhs=w_codes[i][:, n].bitcast(FP8X4),
+                    rhs_scale=w_scales[i][:, n],
+                    start=True,
+                    stop=True,
+                )
+            if j == 0:
+                h_bf[i] = work.tile([P, SLOTS, P, 4], BF16, name="h_wide", align_bytes=64)
+            return bank
+
+        def multiply_h(s, bank):
+            i, j = divmod(s, SLOTS)
+            nc.vector.tensor_tensor(out=h_bf[i][:, j], in0=bank[:].rearrange("p t o -> p o t"), in1=t1_sb[s][:], op=MULT)
+
+        def quantise_h(i):
+            if i < 0:
+                return
+            h_codes[i] = work.tile([P, HALF], U32, name="h_code", bufs=2, align_bytes=64)
+            h_scales[i] = work.tile([P, HALF], U8, name="h_scl", bufs=2, align_bytes=64)
+            nc.vector.quantize_mx(out=h_codes[i][:].bitcast(FP8X4), scales=h_scales[i][:], in_=h_bf[i][:].rearrange("p j o t -> p (j o t)"))
+
+        def product_out(i, m):
+            if i < 0:
+                return
+            b, half = divmod(i, 2)
+            bank = psum.tile([P, HALF], F32, name="out_bank", bufs=1)
+            nc.tensor.matmul_mx(
+                out=bank[:],
+                lhsT=c_words[:, 2 * P * m : 2 * P * (m + 1)].bitcast(FP4X4),
+                lhsT_scale=c_scales[:, P * m : P * (m + 1)],
+                rhs=h_codes[i][:].bitcast(FP8X4),
+                rhs_scale=h_scales[i][:],
+                start=True,
+                stop=True,
+            )
+            t = work.tile([P, HALF], F32, name="out_copy", bufs=4)
+            nc.scalar.copy(out=t[:], in_=bank[:])
+            nc.sync.dma_start(out=out[b, P * m : P * (m + 1), half * HALF : (half + 1) * HALF], in_=t[:])
+
+        scale_row = const.tile([P, CV], F32)
+        nc.scalar.dma_start(out=scale_row[:], in_=w_scale.rearrange("a b c -> (a b c)").partition_broadcast(P))
+        ident = const.tile([P, P], F32)
+        make_identity(nc, ident[:])
+        c_scales = const.tile([P, D], U8, align_bytes=64)
+        nc.vector.memset(c_scales[:].bitcast(I32), 0)
+
+        load_t2(0)
+        load_w(0)
+        a_raw = const.tile([P, 2, R], BF16)
+        nc.sync.dma_start(out=a_raw[:], in_=A.rearrange("(p k) r -> p k r", k=2))
+        load_x1(0)
+        load_w(1)
+        c_words = const.tile([P, 2 * D], U8, align_bytes=64)
+        nc.sync.dma_start(out=c_words[:], in_=C_words[0])
+        for q in range(4):
+            nc.sync.dma_start(out=c_scales[32 * q : 32 * q + 4, :].bitcast(I32), in_=C_scales[0, 4 * q : 4 * q + 4, :].bitcast(I32))
+        for b in range(1, AHEAD):
+            load_sample(b)
+
+        a_perm = const.tile([P, 2, 4, P], BF16)
+        nc.vector.tensor_copy(out=a_perm[:], in_=a_raw[:].rearrange("p k (m t) -> p k t m", t=4))
+
+        turn_t2(0, 0)
+        turn_t2(0, 1)
+        for j in range(SLOTS):
+            scale_w(0, j)
+        quantise_t2(0)
+        product_t1(0)
+        turn_w(0)
+        scale_w(1, 0)
+        quantise_w(0)
+        scale_w(1, 1)
+        scale_w(1, 2)
+        turn_t2(1, 0)
+
+        for i in range(UNITS):
+            b, half = divmod(i, 2)
+            if half == 0 and b + AHEAD < NB:
+                load_sample(b + AHEAD)
+            s = SLOTS * i
+
+            bank = product_t3(s)
+            product_t1(s + 1)
+            multiply_h(s, bank)
+            scale_w(i + 1, 3)
+
+            bank = product_t3(s + 1)
+            product_t1(s + 2)
+            multiply_h(s + 1, bank)
+            scale_w(i + 2, 0)
+            quantise_h(i - 1)
+
+            turn_w(i + 1)
+            turn_t2(b + 1 + half, 1 - half)
+
+            bank = product_t3(s + 2)
+            product_t1(s + 3)
+            product_out(i - 1, 0)
+            quantise_w(i + 1)
+            multiply_h(s + 2, bank)
+            scale_w(i + 2, 1)
+
+            bank = product_t3(s + 3)
+            product_t1(s + 4)
+            product_out(i - 1, 1)
+            if half == 0:
+                quantise_t2(b + 1)
+            multiply_h(s + 3, bank)
+            scale_w(i + 2, 2)
+
+        quantise_h(UNITS - 1)
+        product_out(UNITS - 1, 0)
+        product_out(UNITS - 1, 1)

@@ -35,7 +35,8 @@ def tile_cptensorproduct_pa_t_w4_kernel(tc, x1, A, t2, w_bytes, w_scale, C_words
         x1_sb, t2_sb, w_sb = {}, {}, {}
         w_bf, w_group, w_codes, w_scales = {}, {}, {}, {}
         t2_group, t2_codes, t2_scales = {}, {}, {}
-        t1_sb, h_bf, h_codes, h_scales, out_sb = {}, {}, {}, {}, {}
+        t1_sb, h_bf, h_codes, h_scales = {}, {}, {}, {}
+        turning = {}
 
         def load_w(i):
             b, half = divmod(i, 2)
@@ -60,36 +61,38 @@ def tile_cptensorproduct_pa_t_w4_kernel(tc, x1, A, t2, w_bytes, w_scale, C_words
             load_x1(b)
             load_w(2 * b + 1)
 
-        def scale_w(i, j):
+        def scale_w(i, first, count):
             if i >= UNITS:
                 return
-            if j == 0:
+            if first == 0:
                 w_bf[i] = work.tile([P, SLOTS, CV], BF16, name="w_wide", align_bytes=64)
-            nc.vector.tensor_tensor(out=w_bf[i][:, j, :], in0=w_sb[i][:, j, :].bitcast(FP8), in1=scale_row[:], op=MULT)
+            j = slice(first, first + count)
+            nc.vector.tensor_tensor(out=w_bf[i][:, j, :], in0=w_sb[i][:, j, :].bitcast(FP8), in1=scale_rows[:, :count, :], op=MULT)
 
-        def turn_pair(src, pair, dst):
+        def turns_w(i, pair):
+            return [("w", i, pair, n) for n in range(4)] if i < UNITS else []
+
+        def turns_t2(b, pair):
+            return [("t2", b, pair, n) for n in range(4)] if b < NB else []
+
+        def turn(step):
+            kind, index, pair, n = step
+            if kind == "w":
+                src, group = w_bf[index], w_group
+            else:
+                src, group = t2_sb[index], t2_group
+            if n == 0:
+                turning["bank"] = psum.tile([P, 2, 2, P], F32, name="turned")
+                if pair == 0:
+                    group[index] = work.tile([P, 4 * HALF], BF16, name=kind + "_grouped", align_bytes=64)
+            bank = turning["bank"]
+            jj, u = divmod(n, 2)
+            first = 256 * (2 * pair + jj)
             words = src[:].rearrange("p j c -> p (j c)").bitcast(F32)
-            bank = psum.tile([P, 2, 2, P], F32, name="turned", bufs=3)
-            for jj in range(2):
-                first = 256 * (2 * pair + jj)
-                for u in range(2):
-                    nc.tensor.transpose(bank[:, jj, u, :], words[:, first + u : first + 256 : 2], ident[:])
-            cols = dst[:].bitcast(F32)[:, 512 * pair : 512 * (pair + 1)]
-            nc.scalar.copy(out=cols.rearrange("p (j r u) -> p j r u", j=2, u=2), in_=bank[:].rearrange("p j u r -> p j r u"))
-
-        def turn_w(i):
-            if i >= UNITS:
-                return
-            w_group[i] = work.tile([P, 4 * HALF], BF16, name="w_grouped", align_bytes=64)
-            for pair in range(2):
-                turn_pair(w_bf[i], pair, w_group[i])
-
-        def turn_t2(b, pair):
-            if b >= NB:
-                return
-            if pair == 0:
-                t2_group[b] = work.tile([P, 4 * R], BF16, name="t2_grouped", bufs=2, align_bytes=64)
-            turn_pair(t2_sb[b], pair, t2_group[b])
+            nc.tensor.transpose(bank[:, jj, u, :], words[:, first + u : first + 256 : 2], ident[:])
+            if n == 3:
+                cols = group[index][:].bitcast(F32)[:, 512 * pair : 512 * (pair + 1)]
+                nc.scalar.copy(out=cols.rearrange("p (j r u) -> p j r u", j=2, u=2), in_=bank[:].rearrange("p j u r -> p j r u"))
 
         def quantise_w(i):
             if i >= UNITS:
@@ -105,12 +108,14 @@ def tile_cptensorproduct_pa_t_w4_kernel(tc, x1, A, t2, w_bytes, w_scale, C_words
             t2_scales[b] = work.tile([P, R], U8, name="t2_scl", bufs=2, align_bytes=64)
             nc.vector.quantize_mx(out=t2_codes[b][:].bitcast(FP8X4), scales=t2_scales[b][:], in_=t2_group[b][:])
 
-        def product_t1(s):
+        def product_t1(s, turns):
             if s >= UNITS * SLOTS:
                 return
             b, block = divmod(s, CO // P)
             bank = psum.tile([P, 4, P], F32, name="t1_bank")
             for t in range(4):
+                if 0 < t <= len(turns):
+                    turn(turns[t - 1])
                 for k in range(2):
                     nc.tensor.matmul(
                         bank[:, t, :],
@@ -119,13 +124,13 @@ def tile_cptensorproduct_pa_t_w4_kernel(tc, x1, A, t2, w_bytes, w_scale, C_words
                         start=(k == 0),
                         stop=(k == 1),
                     )
-            t1_sb[s] = work.tile([P, P, 4], F32, name="t1_copy")
+            t1_sb[s] = work.tile([P, P, 4], F32, name="t1_copy", bufs=5)
             nc.scalar.copy(out=t1_sb[s][:], in_=bank[:].rearrange("p t o -> p o t"))
 
         def product_t3(s):
             i, j = divmod(s, SLOTS)
             b = i // 2
-            bank = psum.tile([P, 4, P], F32, name="t3_bank")
+            bank = psum.tile([P, 4, P], F32, name="t3_bank", bufs=3)
             for t in range(4):
                 m = slice(P * t, P * (t + 1))
                 n = slice(P * j, P * (j + 1))
@@ -149,8 +154,8 @@ def tile_cptensorproduct_pa_t_w4_kernel(tc, x1, A, t2, w_bytes, w_scale, C_words
         def quantise_h(i):
             if i < 0:
                 return
-            h_codes[i] = work.tile([P, HALF], U32, name="h_code", bufs=2, align_bytes=64)
-            h_scales[i] = work.tile([P, HALF], U8, name="h_scl", bufs=2, align_bytes=64)
+            h_codes[i] = work.tile([P, HALF], U32, name="h_code", align_bytes=64)
+            h_scales[i] = work.tile([P, HALF], U8, name="h_scl", align_bytes=64)
             nc.vector.quantize_mx(out=h_codes[i][:].bitcast(FP8X4), scales=h_scales[i][:], in_=h_bf[i][:].rearrange("p j o t -> p (j o t)"))
 
         def product_out(i, m):
@@ -171,77 +176,76 @@ def tile_cptensorproduct_pa_t_w4_kernel(tc, x1, A, t2, w_bytes, w_scale, C_words
             nc.scalar.copy(out=t[:], in_=bank[:])
             nc.sync.dma_start(out=out[b, P * m : P * (m + 1), half * HALF : (half + 1) * HALF], in_=t[:])
 
-        scale_row = const.tile([P, CV], F32)
-        nc.scalar.dma_start(out=scale_row[:], in_=w_scale.rearrange("a b c -> (a b c)").partition_broadcast(P))
+        scale_rows = const.tile([P, 2, CV], F32)
+        nc.scalar.dma_start(out=scale_rows[:, 0, :], in_=w_scale.rearrange("a b c -> (a b c)").partition_broadcast(P))
         ident = const.tile([P, P], F32)
         make_identity(nc, ident[:])
         c_scales = const.tile([P, D], U8, align_bytes=64)
         nc.vector.memset(c_scales[:].bitcast(I32), 0)
 
-        load_t2(0)
         load_w(0)
+        load_t2(0)
         a_raw = const.tile([P, 2, R], BF16)
         nc.sync.dma_start(out=a_raw[:], in_=A.rearrange("(p k) r -> p k r", k=2))
         load_x1(0)
         load_w(1)
+        load_w(2)
+        load_t2(1)
+        load_x1(1)
+        load_w(3)
         c_words = const.tile([P, 2 * D], U8, align_bytes=64)
         nc.sync.dma_start(out=c_words[:], in_=C_words[0])
         for q in range(4):
             nc.sync.dma_start(out=c_scales[32 * q : 32 * q + 4, :].bitcast(I32), in_=C_scales[0, 4 * q : 4 * q + 4, :].bitcast(I32))
-        for b in range(1, AHEAD):
+        for b in range(2, AHEAD):
             load_sample(b)
 
         a_perm = const.tile([P, 2, 4, P], BF16)
-        nc.vector.tensor_copy(out=a_perm[:], in_=a_raw[:].rearrange("p k (m t) -> p k t m", t=4))
+        nc.scalar.copy(out=a_perm[:], in_=a_raw[:].rearrange("p k (m t) -> p k t m", t=4))
 
-        turn_t2(0, 0)
-        turn_t2(0, 1)
         for j in range(SLOTS):
-            scale_w(0, j)
+            scale_w(0, j, 1)
+        nc.scalar.copy(out=scale_rows[:, 1, :], in_=scale_rows[:, 0, :])
+        for step in turns_t2(0, 0) + turns_t2(0, 1) + turns_w(0, 0) + turns_w(0, 1):
+            turn(step)
+        scale_w(1, 0, 2)
         quantise_t2(0)
-        product_t1(0)
-        turn_w(0)
-        scale_w(1, 0)
         quantise_w(0)
-        scale_w(1, 1)
-        scale_w(1, 2)
-        turn_t2(1, 0)
+        scale_w(1, 2, 2)
+        scale_w(2, 0, 2)
+        product_t1(0, [])
+        first_turns = turns_t2(1, 0) + turns_w(1, 0) + turns_w(1, 1)
 
         for i in range(UNITS):
             b, half = divmod(i, 2)
             if half == 0 and b + AHEAD < NB:
                 load_sample(b + AHEAD)
-            s = SLOTS * i
-
-            bank = product_t3(s)
-            product_t1(s + 1)
-            multiply_h(s, bank)
-            scale_w(i + 1, 3)
-
-            bank = product_t3(s + 1)
-            product_t1(s + 2)
-            multiply_h(s + 1, bank)
-            scale_w(i + 2, 0)
-            quantise_h(i - 1)
-
-            turn_w(i + 1)
-            turn_t2(b + 1 + half, 1 - half)
-
-            bank = product_t3(s + 2)
-            product_t1(s + 3)
-            product_out(i - 1, 0)
-            quantise_w(i + 1)
-            multiply_h(s + 2, bank)
-            scale_w(i + 2, 1)
-
-            bank = product_t3(s + 3)
-            product_t1(s + 4)
-            product_out(i - 1, 1)
-            if half == 0:
-                quantise_t2(b + 1)
-            multiply_h(s + 3, bank)
-            scale_w(i + 2, 2)
+            turns = turns_t2(b + 1 + half, 1 - half) + turns_w(i + 2, 0) + turns_w(i + 2, 1)
+            if i == 0:
+                turns = first_turns + turns
+            for j in range(SLOTS):
+                s = SLOTS * i + j
+                bank = product_t3(s)
+                if j < 2:
+                    product_out(i - 2, j)
+                share = len(turns) // SLOTS
+                now = turns[share * j : share * (j + 1)]
+                product_t1(s + 1, now[:3])
+                for step in now[3:]:
+                    turn(step)
+                if j == 1:
+                    quantise_w(i + 1)
+                multiply_h(s, bank)
+                if j == 0:
+                    scale_w(i + 2, 2, 2)
+                if j == 1:
+                    quantise_h(i - 1)
+                if j == 2:
+                    scale_w(i + 3, 0, 2)
+                if j == 3 and half == 0:
+                    quantise_t2(b + 1)
 
         quantise_h(UNITS - 1)
-        product_out(UNITS - 1, 0)
-        product_out(UNITS - 1, 1)
+        for i in (UNITS - 2, UNITS - 1):
+            for m in range(2):
+                product_out(i, m)

@@ -20,14 +20,15 @@ P = 128
 HALF = 512
 UNITS = NB * CO // HALF
 SLOTS = HALF // P
-AHEAD = 3
+LEAD = 3
+AHEAD = 4
 
 
 def tile_cptensorproduct_pa_t_w4_kernel(tc, x1, A, t2, w_bytes, w_scale, C_words, C_scales, out):
     nc = tc.nc
     with ExitStack() as ctx:
         const = ctx.enter_context(tc.tile_pool(name="const", bufs=1))
-        loads = ctx.enter_context(tc.tile_pool(name="loads", bufs=4))
+        loads = ctx.enter_context(tc.tile_pool(name="loads", bufs=6))
         work = ctx.enter_context(tc.tile_pool(name="work", bufs=3))
         psum = ctx.enter_context(tc.psum_pool(name="psum", bufs=2))
         ctx.enter_context(tc.manual_schedule())
@@ -36,11 +37,11 @@ def tile_cptensorproduct_pa_t_w4_kernel(tc, x1, A, t2, w_bytes, w_scale, C_words
         w_bf, w_group, w_codes, w_scales = {}, {}, {}, {}
         t2_group, t2_codes, t2_scales = {}, {}, {}
         t1_sb, h_bf, h_codes, h_scales = {}, {}, {}, {}
-        turning = {}
+        w_last, turning = {}, {}
 
         def load_w(i):
             b, half = divmod(i, 2)
-            t = loads.tile([P, SLOTS, CV], U8, name="w_raw", bufs=8)
+            t = loads.tile([P, SLOTS, CV], U8, name="w_raw", bufs=12)
             rows = w_bytes[b, half * HALF : (half + 1) * HALF, :]
             nc.sync.dma_start(out=t[:], in_=rows.rearrange("(j p) c -> p j c", p=P))
             w_sb[i] = t
@@ -64,19 +65,35 @@ def tile_cptensorproduct_pa_t_w4_kernel(tc, x1, A, t2, w_bytes, w_scale, C_words
         def scale_w(i, first, count):
             if i >= UNITS:
                 return
-            if first == 0:
+            if i not in w_bf:
                 w_bf[i] = work.tile([P, SLOTS, CV], BF16, name="w_wide", align_bytes=64)
             j = slice(first, first + count)
             nc.vector.tensor_tensor(out=w_bf[i][:, j, :], in0=w_sb[i][:, j, :].bitcast(FP8), in1=scale_rows[:, :count, :], op=MULT)
 
+        def widen_last(i):
+            if i >= UNITS:
+                return
+            w_last[i] = work.tile([P, CV], BF16, name="w_last_wide")
+            nc.scalar.copy(out=w_last[i][:], in_=w_sb[i][:, SLOTS - 1, :].bitcast(FP8))
+
+        def scale_last(i):
+            if i >= UNITS:
+                return
+            if i not in w_bf:
+                w_bf[i] = work.tile([P, SLOTS, CV], BF16, name="w_wide", align_bytes=64)
+            nc.vector.memset(w_bf[i][:, SLOTS - 1, 0:2], 0.0)
+            nc.gpsimd.tensor_tensor(out=w_bf[i][:, SLOTS - 1, :], in0=w_last[i][:], in1=scale_rows[:, 0, :], op=MULT)
+
         def turns_w(i, pair):
-            return [("w", i, pair, n) for n in range(4)] if i < UNITS else []
+            return [("w", i, pair, n) for n in range(4)]
 
         def turns_t2(b, pair):
-            return [("t2", b, pair, n) for n in range(4)] if b < NB else []
+            return [("t2", b, pair, n) for n in range(4)]
 
         def turn(step):
             kind, index, pair, n = step
+            if index >= (UNITS if kind == "w" else NB):
+                return
             if kind == "w":
                 src, group = w_bf[index], w_group
             else:
@@ -91,8 +108,9 @@ def tile_cptensorproduct_pa_t_w4_kernel(tc, x1, A, t2, w_bytes, w_scale, C_words
             words = src[:].rearrange("p j c -> p (j c)").bitcast(F32)
             nc.tensor.transpose(bank[:, jj, u, :], words[:, first + u : first + 256 : 2], ident[:])
             if n == 3:
+                copy = nc.vector.tensor_copy if kind == "t2" and index == 0 else nc.scalar.copy
                 cols = group[index][:].bitcast(F32)[:, 512 * pair : 512 * (pair + 1)]
-                nc.scalar.copy(out=cols.rearrange("p (j r u) -> p j r u", j=2, u=2), in_=bank[:].rearrange("p j u r -> p j r u"))
+                copy(out=cols.rearrange("p (j r u) -> p j r u", j=2, u=2), in_=bank[:].rearrange("p j u r -> p j r u"))
 
         def quantise_w(i):
             if i >= UNITS:
@@ -110,6 +128,8 @@ def tile_cptensorproduct_pa_t_w4_kernel(tc, x1, A, t2, w_bytes, w_scale, C_words
 
         def product_t1(s, turns):
             if s >= UNITS * SLOTS:
+                for step in turns:
+                    turn(step)
                 return
             b, block = divmod(s, CO // P)
             bank = psum.tile([P, 4, P], F32, name="t1_bank")
@@ -124,13 +144,15 @@ def tile_cptensorproduct_pa_t_w4_kernel(tc, x1, A, t2, w_bytes, w_scale, C_words
                         start=(k == 0),
                         stop=(k == 1),
                     )
-            t1_sb[s] = work.tile([P, P, 4], F32, name="t1_copy", bufs=5)
+            for step in turns[3:]:
+                turn(step)
+            t1_sb[s] = work.tile([P, P, 4], F32, name="t1_copy", bufs=7)
             nc.scalar.copy(out=t1_sb[s][:], in_=bank[:].rearrange("p t o -> p o t"))
 
         def product_t3(s):
             i, j = divmod(s, SLOTS)
             b = i // 2
-            bank = psum.tile([P, 4, P], F32, name="t3_bank", bufs=3)
+            bank = psum.tile([P, 4, P], F32, name="t3_bank")
             for t in range(4):
                 m = slice(P * t, P * (t + 1))
                 n = slice(P * j, P * (j + 1))
@@ -151,30 +173,38 @@ def tile_cptensorproduct_pa_t_w4_kernel(tc, x1, A, t2, w_bytes, w_scale, C_words
             i, j = divmod(s, SLOTS)
             nc.vector.tensor_tensor(out=h_bf[i][:, j], in0=bank[:].rearrange("p t o -> p o t"), in1=t1_sb[s][:], op=MULT)
 
-        def quantise_h(i):
+        def quantise_h(i, first=0, width=HALF):
             if i < 0:
                 return
-            h_codes[i] = work.tile([P, HALF], U32, name="h_code", align_bytes=64)
-            h_scales[i] = work.tile([P, HALF], U8, name="h_scl", align_bytes=64)
-            nc.vector.quantize_mx(out=h_codes[i][:].bitcast(FP8X4), scales=h_scales[i][:], in_=h_bf[i][:].rearrange("p j o t -> p (j o t)"))
+            if first == 0:
+                h_codes[i] = work.tile([P, HALF], U32, name="h_code", align_bytes=64)
+                h_scales[i] = work.tile([P, HALF], U8, name="h_scl", align_bytes=64)
+            n = slice(first, first + width)
+            wide = h_bf[i][:].rearrange("p j o t -> p (j o t)")
+            nc.vector.quantize_mx(out=h_codes[i][:, n].bitcast(FP8X4), scales=h_scales[i][:, n], in_=wide[:, 4 * first : 4 * (first + width)])
 
-        def product_out(i, m):
+        def product_out(i, m, first=0, width=HALF, tag="out_bank", engine="scalar"):
             if i < 0:
                 return
             b, half = divmod(i, 2)
-            bank = psum.tile([P, HALF], F32, name="out_bank", bufs=1)
+            n = slice(first, first + width)
+            bank = psum.tile([P, HALF], F32, name=tag)
             nc.tensor.matmul_mx(
-                out=bank[:],
+                out=bank[:, :width],
                 lhsT=c_words[:, 2 * P * m : 2 * P * (m + 1)].bitcast(FP4X4),
                 lhsT_scale=c_scales[:, P * m : P * (m + 1)],
-                rhs=h_codes[i][:].bitcast(FP8X4),
-                rhs_scale=h_scales[i][:],
+                rhs=h_codes[i][:, n].bitcast(FP8X4),
+                rhs_scale=h_scales[i][:, n],
                 start=True,
                 stop=True,
             )
-            t = work.tile([P, HALF], F32, name="out_copy", bufs=4)
-            nc.scalar.copy(out=t[:], in_=bank[:])
-            nc.sync.dma_start(out=out[b, P * m : P * (m + 1), half * HALF : (half + 1) * HALF], in_=t[:])
+            t = work.tile([P, HALF], F32, name="out_copy", bufs=8)
+            if engine == "vector":
+                nc.vector.tensor_copy(out=t[:, :width], in_=bank[:, :width])
+            else:
+                nc.scalar.copy(out=t[:, :width], in_=bank[:, :width])
+            cols = half * HALF + first
+            nc.sync.dma_start(out=out[b, P * m : P * (m + 1), cols : cols + width], in_=t[:, :width])
 
         scale_rows = const.tile([P, 2, CV], F32)
         nc.scalar.dma_start(out=scale_rows[:, 0, :], in_=w_scale.rearrange("a b c -> (a b c)").partition_broadcast(P))
@@ -200,52 +230,61 @@ def tile_cptensorproduct_pa_t_w4_kernel(tc, x1, A, t2, w_bytes, w_scale, C_words
         for b in range(2, AHEAD):
             load_sample(b)
 
+        for step in turns_t2(0, 0) + turns_t2(0, 1):
+            turn(step)
         a_perm = const.tile([P, 2, 4, P], BF16)
         nc.scalar.copy(out=a_perm[:], in_=a_raw[:].rearrange("p k (m t) -> p k t m", t=4))
-
+        nc.scalar.copy(out=scale_rows[:, 1, :], in_=scale_rows[:, 0, :])
         for j in range(SLOTS):
             scale_w(0, j, 1)
-        nc.scalar.copy(out=scale_rows[:, 1, :], in_=scale_rows[:, 0, :])
-        for step in turns_t2(0, 0) + turns_t2(0, 1) + turns_w(0, 0) + turns_w(0, 1):
+        for step in turns_w(0, 0) + turns_w(0, 1):
             turn(step)
-        scale_w(1, 0, 2)
+        for s in range(LEAD):
+            product_t1(s, [])
+        widen_last(2)
         quantise_t2(0)
+        scale_w(1, 0, 2)
+        for step in turns_t2(1, 0) + turns_w(1, 0):
+            turn(step)
         quantise_w(0)
         scale_w(1, 2, 2)
-        scale_w(2, 0, 2)
-        product_t1(0, [])
-        first_turns = turns_t2(1, 0) + turns_w(1, 0) + turns_w(1, 1)
 
+        banks = {}
         for i in range(UNITS):
             b, half = divmod(i, 2)
             if half == 0 and b + AHEAD < NB:
                 load_sample(b + AHEAD)
-            turns = turns_t2(b + 1 + half, 1 - half) + turns_w(i + 2, 0) + turns_w(i + 2, 1)
-            if i == 0:
-                turns = first_turns + turns
-            for j in range(SLOTS):
-                s = SLOTS * i + j
-                bank = product_t3(s)
-                if j < 2:
-                    product_out(i - 2, j)
-                share = len(turns) // SLOTS
-                now = turns[share * j : share * (j + 1)]
-                product_t1(s + 1, now[:3])
-                for step in now[3:]:
-                    turn(step)
-                if j == 1:
-                    quantise_w(i + 1)
-                multiply_h(s, bank)
-                if j == 0:
-                    scale_w(i + 2, 2, 2)
-                if j == 1:
+            s = SLOTS * i
+            turns = turns_w(i + 1, 1) + turns_t2(b + 1 + half, 1 - half) + turns_w(i + 2, 0)
+            share = 3
+            for k in range(2):
+                for j in (2 * k, 2 * k + 1):
+                    banks[j] = product_t3(s + j)
+                product_out(i - 2, k)
+                for j in (2 * k, 2 * k + 1):
+                    product_t1(s + LEAD + j, turns[share * j : share * (j + 1)])
+                if k == 0:
+                    widen_last(i + 3)
+                else:
+                    scale_last(i + 2)
+                for j in (2 * k, 2 * k + 1):
+                    multiply_h(s + j, banks[j])
+                if k == 0:
+                    scale_w(i + 2, 0, 2)
                     quantise_h(i - 1)
-                if j == 2:
-                    scale_w(i + 3, 0, 2)
-                if j == 3 and half == 0:
-                    quantise_t2(b + 1)
+                    quantise_w(i + 1)
+                    if i == UNITS - 1:
+                        quantise_h(i, 0, HALF // 2)
+                else:
+                    scale_w(i + 2, 2, 1)
+                    if half == 0:
+                        quantise_t2(b + 1)
 
-        quantise_h(UNITS - 1)
-        for i in (UNITS - 2, UNITS - 1):
-            for m in range(2):
-                product_out(i, m)
+        i, n = UNITS - 1, HALF // 2
+        product_out(i - 1, 0)
+        product_out(i - 1, 1)
+        product_out(i, 0, 0, n, tag="t3_bank")
+        product_out(i, 1, 0, n, tag="t3_bank")
+        quantise_h(i, n, n)
+        product_out(i, 0, n, n)
+        product_out(i, 1, n, n, engine="vector")

@@ -17,206 +17,193 @@ FP4X4 = mybir.dt.float4_e2m1fn_x4
 MULT = mybir.AluOpType.mult
 
 P = 128
+PACK = 4
 HALF = 512
+BLOCKS = HALF // P
 UNITS = NB * CO // HALF
-SLOTS = HALF // P
-LEAD = 3
-AHEAD = 4
+LAST = UNITS - 1
+W_COLS = BLOCKS * CV
+
+PAIR = 2 * CV
+OVERLAP = 16
+SHARE = slice(W_COLS - 448, W_COLS)
+SHARE_COLS = SHARE.stop - SHARE.start
+FIRST_SHARED = 2
+T1_LEAD = 3
+TURN_STEPS = 3
 
 
 def tile_cptensorproduct_pa_t_w4_kernel(tc, x1, A, t2, w_bytes, w_scale, C_words, C_scales, out):
     nc = tc.nc
     with ExitStack() as ctx:
         const = ctx.enter_context(tc.tile_pool(name="const", bufs=1))
-        loads = ctx.enter_context(tc.tile_pool(name="loads", bufs=6))
+        loads = ctx.enter_context(tc.tile_pool(name="loads", bufs=NB))
         work = ctx.enter_context(tc.tile_pool(name="work", bufs=3))
         psum = ctx.enter_context(tc.psum_pool(name="psum", bufs=2))
         ctx.enter_context(tc.manual_schedule())
 
-        x1_sb, t2_sb, w_sb = {}, {}, {}
-        w_bf, w_group, w_codes, w_scales = {}, {}, {}, {}
-        t2_group, t2_codes, t2_scales = {}, {}, {}
-        t1_sb, h_bf, h_codes, h_scales = {}, {}, {}, {}
-        w_last, turning = {}, {}
+        x1_raw, t2_raw, w_raw = {}, {}, {}
+        w_share, w_bf = {}, {}
+        t2_turned, t2_codes, t2_scales = {}, {}, {}
+        t1_sb, joint, codes, scales = {}, {}, {}, {}
+        current = {}
 
         def load_w(i):
             b, half = divmod(i, 2)
-            t = loads.tile([P, SLOTS, CV], U8, name="w_raw", bufs=12)
-            rows = w_bytes[b, half * HALF : (half + 1) * HALF, :]
-            nc.sync.dma_start(out=t[:], in_=rows.rearrange("(j p) c -> p j c", p=P))
-            w_sb[i] = t
+            w_raw[i] = loads.tile([P, W_COLS], U8, name="w_raw_bytes", bufs=UNITS)
+            rows = w_bytes[b, half * HALF : (half + 1) * HALF, :].rearrange("(j p) c -> p j c", p=P)
+            nc.sync.dma_start(out=w_raw[i][:].rearrange("p (j c) -> p j c", j=BLOCKS), in_=rows)
 
         def load_t2(b):
-            t = loads.tile([P, 4, CV], BF16, name="t2_raw")
-            nc.sync.dma_start(out=t[:], in_=t2[b].rearrange("(m t) c -> m t c", t=4))
-            t2_sb[b] = t
+            t2_raw[b] = loads.tile([P, PACK * CV], BF16, name="t2_rows")
+            nc.sync.dma_start(out=t2_raw[b][:], in_=t2[b].rearrange("(m t) c -> m (t c)", t=PACK))
 
         def load_x1(b):
-            t = loads.tile([P, 2, CO], BF16, name="x1_raw")
-            nc.sync.dma_start(out=t[:], in_=x1[b].rearrange("(p k) o -> p k o", k=2))
-            x1_sb[b] = t
-
-        def load_sample(b):
-            load_w(2 * b)
-            load_t2(b)
-            load_x1(b)
-            load_w(2 * b + 1)
+            x1_raw[b] = loads.tile([P, 2, CO], BF16, name="x1_rows")
+            nc.sync.dma_start(out=x1_raw[b][:], in_=x1[b].rearrange("(p k) o -> p k o", k=2))
 
         def scale_w(i, first, count):
-            if i >= UNITS:
+            if i > LAST:
                 return
             if i not in w_bf:
-                w_bf[i] = work.tile([P, SLOTS, CV], BF16, name="w_wide", align_bytes=64)
-            j = slice(first, first + count)
-            nc.vector.tensor_tensor(out=w_bf[i][:, j, :], in0=w_sb[i][:, j, :].bitcast(FP8), in1=scale_rows[:, :count, :], op=MULT)
+                w_bf[i] = work.tile([P, W_COLS], BF16, name="w_scaled", align_bytes=64)
+            cols = slice(first, first + count)
+            scales = scale_rows[:, first % CV : first % CV + count]
+            nc.vector.tensor_tensor(out=w_bf[i][:, cols], in0=w_raw[i][:, cols].bitcast(FP8), in1=scales, op=MULT)
 
-        def widen_last(i):
-            if i >= UNITS:
+        def widen_share(i):
+            if i > LAST:
                 return
-            w_last[i] = work.tile([P, CV], BF16, name="w_last_wide")
-            nc.scalar.copy(out=w_last[i][:], in_=w_sb[i][:, SLOTS - 1, :].bitcast(FP8))
+            w_share[i] = work.tile([P, SHARE_COLS], BF16, name="w_widened")
+            nc.scalar.copy(out=w_share[i][:], in_=w_raw[i][:, SHARE].bitcast(FP8))
 
-        def scale_last(i):
-            if i >= UNITS:
+        def scale_share(i):
+            if i > LAST:
                 return
-            if i not in w_bf:
-                w_bf[i] = work.tile([P, SLOTS, CV], BF16, name="w_wide", align_bytes=64)
-            nc.vector.memset(w_bf[i][:, SLOTS - 1, 0:2], 0.0)
-            nc.gpsimd.tensor_tensor(out=w_bf[i][:, SLOTS - 1, :], in0=w_last[i][:], in1=scale_rows[:, 0, :], op=MULT)
+            scales = scale_rows[:, SHARE.start % CV : SHARE.start % CV + SHARE_COLS]
+            nc.gpsimd.tensor_tensor(out=w_bf[i][:, SHARE], in0=w_share[i][:], in1=scales, op=MULT)
 
-        def turns_w(i, pair):
-            return [("w", i, pair, n) for n in range(4)]
-
-        def turns_t2(b, pair):
-            return [("t2", b, pair, n) for n in range(4)]
+        def turns(kind, index, pair):
+            return [(kind, index, pair, n) for n in range(4)]
 
         def turn(step):
             kind, index, pair, n = step
             if index >= (UNITS if kind == "w" else NB):
                 return
-            if kind == "w":
-                src, group = w_bf[index], w_group
-            else:
-                src, group = t2_sb[index], t2_group
             if n == 0:
-                turning["bank"] = psum.tile([P, 2, 2, P], F32, name="turned")
-                if pair == 0:
-                    group[index] = work.tile([P, 4 * HALF], BF16, name=kind + "_grouped", align_bytes=64)
-            bank = turning["bank"]
-            jj, u = divmod(n, 2)
-            first = 256 * (2 * pair + jj)
-            words = src[:].rearrange("p j c -> p (j c)").bitcast(F32)
-            nc.tensor.transpose(bank[:, jj, u, :], words[:, first + u : first + 256 : 2], ident[:])
+                current["bank"] = psum.tile([P, 2, 2, P], F32, name="turn_bank")
+            bank = current["bank"]
+            if kind == "t2" and index not in t2_turned:
+                t2_turned[index] = work.tile([P, PACK * R], BF16, name="t2_grouped", align_bytes=64)
+            turned = joint_tile(index - 1)[:, 1, :] if kind == "w" else t2_turned[index][:]
+            words = (w_bf if kind == "w" else t2_raw)[index][:].bitcast(F32)
+            j, u = divmod(n, 2)
+            first = (2 * pair + j) * CV // 2
+            nc.tensor.transpose(bank[:, j, u, :], words[:, first + u : first + CV // 2 : 2], ident[:])
             if n == 3:
-                copy = nc.vector.tensor_copy if kind == "t2" and index == 0 else nc.scalar.copy
-                cols = group[index][:].bitcast(F32)[:, 512 * pair : 512 * (pair + 1)]
-                copy(out=cols.rearrange("p (j r u) -> p j r u", j=2, u=2), in_=bank[:].rearrange("p j u r -> p j r u"))
+                group = turned.bitcast(F32)[:, 4 * P * pair : 4 * P * (pair + 1)]
+                nc.scalar.copy(out=group.rearrange("p (j r u) -> p j r u", j=2, u=2), in_=bank[:].rearrange("p j u r -> p j r u"))
 
-        def quantise_w(i):
-            if i >= UNITS:
-                return
-            w_codes[i] = work.tile([P, HALF], U32, name="w_code", align_bytes=64)
-            w_scales[i] = work.tile([P, HALF], U8, name="w_scl", align_bytes=64)
-            nc.vector.quantize_mx(out=w_codes[i][:].bitcast(FP8X4), scales=w_scales[i][:], in_=w_group[i][:])
+        def joint_tile(i):
+            if i not in joint:
+                joint[i] = work.tile([P, 2, PACK * HALF], BF16, name="h_and_w_grouped", align_bytes=64)
+            return joint[i]
 
-        def quantise_t2(b):
+        def joint_codes(i):
+            if i not in codes:
+                codes[i] = work.tile([P, 2, HALF], U32, name="h_and_w_code", align_bytes=64)
+                scales[i] = work.tile([P, 2, HALF], U8, name="h_and_w_code_scale", align_bytes=64)
+            return codes[i][:].rearrange("p x n -> p (x n)"), scales[i][:].rearrange("p x n -> p (x n)")
+
+        def quantise(i, first, count):
+            code, scale = joint_codes(i)
+            n = slice(first, first + count)
+            wide = joint_tile(i)[:].rearrange("p x n -> p (x n)")[:, PACK * first : PACK * (first + count)]
+            nc.vector.quantize_mx(out=code[:, n].bitcast(FP8X4), scales=scale[:, n], in_=wide)
+
+        def quantise_t2(b, pair):
             if b >= NB:
                 return
-            t2_codes[b] = work.tile([P, R], U32, name="t2_code", bufs=2, align_bytes=64)
-            t2_scales[b] = work.tile([P, R], U8, name="t2_scl", bufs=2, align_bytes=64)
-            nc.vector.quantize_mx(out=t2_codes[b][:].bitcast(FP8X4), scales=t2_scales[b][:], in_=t2_group[b][:])
+            if pair == 0:
+                t2_codes[b] = work.tile([P, R], U32, name="t2_code", align_bytes=64)
+                t2_scales[b] = work.tile([P, R], U8, name="t2_code_scale", align_bytes=64)
+            m = slice(2 * P * pair, 2 * P * (pair + 1))
+            wide = t2_turned[b][:, PACK * m.start : PACK * m.stop]
+            nc.vector.quantize_mx(out=t2_codes[b][:, m].bitcast(FP8X4), scales=t2_scales[b][:, m], in_=wide)
 
-        def product_t1(s, turns):
-            if s >= UNITS * SLOTS:
-                for step in turns:
+        def product_t1(s, steps):
+            if s < UNITS * BLOCKS:
+                b, block = divmod(s, CO // P)
+                bank = psum.tile([P, PACK, P], F32, name="t1_bank")
+                for t in range(PACK):
+                    if 0 < t <= len(steps):
+                        turn(steps[t - 1])
+                    for k in range(2):
+                        rhs = x1_raw[b][:, k, P * block : P * (block + 1)]
+                        nc.tensor.matmul(bank[:, t, :], lhsT=a_perm[:, k, t, :], rhs=rhs, start=(k == 0), stop=(k == 1))
+                t1_sb[s] = work.tile([P, P, PACK], F32, name="t1_copy", bufs=T1_LEAD + 4)
+                nc.scalar.copy(out=t1_sb[s][:], in_=bank[:].rearrange("p t o -> p o t"))
+            else:
+                for step in steps:
                     turn(step)
-                return
-            b, block = divmod(s, CO // P)
-            bank = psum.tile([P, 4, P], F32, name="t1_bank")
-            for t in range(4):
-                if 0 < t <= len(turns):
-                    turn(turns[t - 1])
-                for k in range(2):
-                    nc.tensor.matmul(
-                        bank[:, t, :],
-                        lhsT=a_perm[:, k, t, :],
-                        rhs=x1_sb[b][:, k, P * block : P * (block + 1)],
-                        start=(k == 0),
-                        stop=(k == 1),
-                    )
-            for step in turns[3:]:
-                turn(step)
-            t1_sb[s] = work.tile([P, P, 4], F32, name="t1_copy", bufs=7)
-            nc.scalar.copy(out=t1_sb[s][:], in_=bank[:].rearrange("p t o -> p o t"))
 
         def product_t3(s):
-            i, j = divmod(s, SLOTS)
+            i, j = divmod(s, BLOCKS)
             b = i // 2
-            bank = psum.tile([P, 4, P], F32, name="t3_bank")
-            for t in range(4):
+            bank = psum.tile([P, PACK, P], F32, name="t3_bank")
+            n = slice(P * j, P * (j + 1))
+            for t in range(PACK):
                 m = slice(P * t, P * (t + 1))
-                n = slice(P * j, P * (j + 1))
                 nc.tensor.matmul_mx(
                     out=bank[:, t, :],
                     lhsT=t2_codes[b][:, m].bitcast(FP8X4),
                     lhsT_scale=t2_scales[b][:, m],
-                    rhs=w_codes[i][:, n].bitcast(FP8X4),
-                    rhs_scale=w_scales[i][:, n],
+                    rhs=codes[i - 1][:, 1, n].bitcast(FP8X4),
+                    rhs_scale=scales[i - 1][:, 1, n],
                     start=True,
                     stop=True,
                 )
-            if j == 0:
-                h_bf[i] = work.tile([P, SLOTS, P, 4], BF16, name="h_wide", align_bytes=64)
             return bank
 
         def multiply_h(s, bank):
-            i, j = divmod(s, SLOTS)
-            nc.vector.tensor_tensor(out=h_bf[i][:, j], in0=bank[:].rearrange("p t o -> p o t"), in1=t1_sb[s][:], op=MULT)
+            i, j = divmod(s, BLOCKS)
+            h = joint_tile(i + 1)[:, 0, PACK * P * j : PACK * P * (j + 1)].rearrange("p (o t) -> p o t", t=PACK)
+            nc.vector.tensor_tensor(out=h, in0=bank[:].rearrange("p t o -> p o t"), in1=t1_sb[s][:], op=MULT)
 
-        def quantise_h(i, first=0, width=HALF):
-            if i < 0:
-                return
-            if first == 0:
-                h_codes[i] = work.tile([P, HALF], U32, name="h_code", align_bytes=64)
-                h_scales[i] = work.tile([P, HALF], U8, name="h_scl", align_bytes=64)
-            n = slice(first, first + width)
-            wide = h_bf[i][:].rearrange("p j o t -> p (j o t)")
-            nc.vector.quantize_mx(out=h_codes[i][:, n].bitcast(FP8X4), scales=h_scales[i][:, n], in_=wide[:, 4 * first : 4 * (first + width)])
-
-        def product_out(i, m, first=0, width=HALF, tag="out_bank", engine="scalar"):
+        def product_out(i, m, first=0, count=HALF, bank_name="out_bank", copy=nc.scalar.copy):
             if i < 0:
                 return
             b, half = divmod(i, 2)
-            n = slice(first, first + width)
-            bank = psum.tile([P, HALF], F32, name=tag)
+            n = slice(first, first + count)
+            bank = psum.tile([P, HALF], F32, name=bank_name)
             nc.tensor.matmul_mx(
-                out=bank[:, :width],
+                out=bank[:, :count],
                 lhsT=c_words[:, 2 * P * m : 2 * P * (m + 1)].bitcast(FP4X4),
                 lhsT_scale=c_scales[:, P * m : P * (m + 1)],
-                rhs=h_codes[i][:, n].bitcast(FP8X4),
-                rhs_scale=h_scales[i][:, n],
+                rhs=codes[i + 1][:, 0, n].bitcast(FP8X4),
+                rhs_scale=scales[i + 1][:, 0, n],
                 start=True,
                 stop=True,
             )
-            t = work.tile([P, HALF], F32, name="out_copy", bufs=8)
-            if engine == "vector":
-                nc.vector.tensor_copy(out=t[:, :width], in_=bank[:, :width])
-            else:
-                nc.scalar.copy(out=t[:, :width], in_=bank[:, :width])
-            cols = half * HALF + first
-            nc.sync.dma_start(out=out[b, P * m : P * (m + 1), cols : cols + width], in_=t[:, :width])
+            result = work.tile([P, HALF], F32, name="out_copy", bufs=8)
+            copy(out=result[:, :count], in_=bank[:, :count])
+            col = half * HALF + first
+            nc.sync.dma_start(out=out[b, P * m : P * (m + 1), col : col + count], in_=result[:, :count])
 
-        scale_rows = const.tile([P, 2, CV], F32)
-        nc.scalar.dma_start(out=scale_rows[:, 0, :], in_=w_scale.rearrange("a b c -> (a b c)").partition_broadcast(P))
+        scale_row = const.tile([P, CV], F32)
+        nc.vector.memset(scale_row[:], 0.0)
+        nc.scalar.dma_start(out=scale_row[0:1, :], in_=w_scale[0])
+        ones = const.tile([P, P], F32)
+        nc.vector.memset(ones[:], 1.0)
         ident = const.tile([P, P], F32)
         make_identity(nc, ident[:])
         c_scales = const.tile([P, D], U8, align_bytes=64)
         nc.vector.memset(c_scales[:].bitcast(I32), 0)
 
         load_w(0)
-        load_t2(0)
         a_raw = const.tile([P, 2, R], BF16)
         nc.sync.dma_start(out=a_raw[:], in_=A.rearrange("(p k) r -> p k r", k=2))
+        load_t2(0)
         load_x1(0)
         load_w(1)
         load_w(2)
@@ -226,65 +213,76 @@ def tile_cptensorproduct_pa_t_w4_kernel(tc, x1, A, t2, w_bytes, w_scale, C_words
         c_words = const.tile([P, 2 * D], U8, align_bytes=64)
         nc.sync.dma_start(out=c_words[:], in_=C_words[0])
         for q in range(4):
-            nc.sync.dma_start(out=c_scales[32 * q : 32 * q + 4, :].bitcast(I32), in_=C_scales[0, 4 * q : 4 * q + 4, :].bitcast(I32))
-        for b in range(2, AHEAD):
-            load_sample(b)
+            rows = C_scales[0, 4 * q : 4 * q + 4, :].bitcast(I32)
+            nc.sync.dma_start(out=c_scales[32 * q : 32 * q + 4, :].bitcast(I32), in_=rows)
+        for b in range(2, NB):
+            load_w(2 * b)
+            load_t2(b)
+            load_x1(b)
+            load_w(2 * b + 1)
 
-        for step in turns_t2(0, 0) + turns_t2(0, 1):
+        bank = psum.tile([P, CV], F32, name="out_bank")
+        nc.tensor.matmul(bank[:], lhsT=ones[:], rhs=scale_row[:], start=True, stop=True)
+        scale_rows = const.tile([P, 2 * CV], F32)
+        nc.scalar.copy(out=scale_rows[:, :CV], in_=bank[:])
+        for step in turns("t2", 0, 0) + turns("t2", 0, 1):
             turn(step)
-        a_perm = const.tile([P, 2, 4, P], BF16)
-        nc.scalar.copy(out=a_perm[:], in_=a_raw[:].rearrange("p k (m t) -> p k t m", t=4))
-        nc.scalar.copy(out=scale_rows[:, 1, :], in_=scale_rows[:, 0, :])
-        for j in range(SLOTS):
-            scale_w(0, j, 1)
-        for step in turns_w(0, 0) + turns_w(0, 1):
-            turn(step)
-        for s in range(LEAD):
+        a_perm = const.tile([P, 2, PACK, P], BF16)
+        nc.vector.tensor_copy(out=a_perm[:], in_=a_raw[:].rearrange("p k (m t) -> p k t m", t=PACK))
+        for s in range(2):
             product_t1(s, [])
-        widen_last(2)
-        quantise_t2(0)
-        scale_w(1, 0, 2)
-        for step in turns_t2(1, 0) + turns_w(1, 0):
+        nc.scalar.copy(out=scale_rows[:, CV:], in_=bank[:])
+        for j in range(BLOCKS):
+            scale_w(0, CV * j, CV)
+        for step in turns("w", 0, 0) + turns("w", 0, 1):
             turn(step)
-        quantise_w(0)
-        scale_w(1, 2, 2)
+        for s in range(2, T1_LEAD):
+            product_t1(s, [])
+        widen_share(FIRST_SHARED)
+        quantise_t2(0, 0)
+        quantise_t2(0, 1)
+        scale_w(1, 0, 2 * CV)
+        for step in turns("t2", 1, 0) + turns("w", 1, 0):
+            turn(step)
+        quantise(-1, HALF, HALF)
+        quantise_t2(1, 0)
+        scale_w(1, 2 * CV, 2 * CV)
+        scale_w(2, PAIR, SHARE.start + OVERLAP - PAIR)
+        scale_share(2)
 
-        banks = {}
         for i in range(UNITS):
             b, half = divmod(i, 2)
-            if half == 0 and b + AHEAD < NB:
-                load_sample(b + AHEAD)
-            s = SLOTS * i
-            turns = turns_w(i + 1, 1) + turns_t2(b + 1 + half, 1 - half) + turns_w(i + 2, 0)
-            share = 3
+            first_turns = turns("w", i + 1, 1) if i < LAST - 1 else []
+            middle_turns = turns("t2", b + 1 + half, 1 - half) if i < LAST - 2 else turns("w", i + 2, 1)
+            steps = first_turns + middle_turns + turns("w", i + 2, 0)
             for k in range(2):
-                for j in (2 * k, 2 * k + 1):
-                    banks[j] = product_t3(s + j)
+                pair = (BLOCKS * i + 2 * k, BLOCKS * i + 2 * k + 1)
+                banks = [product_t3(s) for s in pair]
                 product_out(i - 2, k)
-                for j in (2 * k, 2 * k + 1):
-                    product_t1(s + LEAD + j, turns[share * j : share * (j + 1)])
+                for s in pair:
+                    first = TURN_STEPS * (s % BLOCKS)
+                    product_t1(s + T1_LEAD, steps[first : first + TURN_STEPS])
+                for s, bank in zip(pair, banks):
+                    multiply_h(s, bank)
                 if k == 0:
-                    widen_last(i + 3)
+                    widen_share(i + 3)
+                    scale_w(i + 2, 0, PAIR)
+                    if i > 0:
+                        quantise(i, 0, HALF)
+                    if i < LAST:
+                        quantise(i, HALF, HALF)
+                    else:
+                        quantise(LAST + 1, 0, HALF // 2)
                 else:
-                    scale_last(i + 2)
-                for j in (2 * k, 2 * k + 1):
-                    multiply_h(s + j, banks[j])
-                if k == 0:
-                    scale_w(i + 2, 0, 2)
-                    quantise_h(i - 1)
-                    quantise_w(i + 1)
-                    if i == UNITS - 1:
-                        quantise_h(i, 0, HALF // 2)
-                else:
-                    scale_w(i + 2, 2, 1)
-                    if half == 0:
-                        quantise_t2(b + 1)
+                    scale_w(i + 3, PAIR, SHARE.start + OVERLAP - PAIR)
+                    quantise_t2(b + 1 + half, 1 - half)
+                    scale_share(i + 3)
 
-        i, n = UNITS - 1, HALF // 2
-        product_out(i - 1, 0)
-        product_out(i - 1, 1)
-        product_out(i, 0, 0, n, tag="t3_bank")
-        product_out(i, 1, 0, n, tag="t3_bank")
-        quantise_h(i, n, n)
-        product_out(i, 0, n, n)
-        product_out(i, 1, n, n, engine="vector")
+        n = HALF // 2
+        product_out(LAST - 1, 0, bank_name="t1_bank")
+        for m in range(2):
+            product_out(LAST, m, 0, n, bank_name="t3_bank")
+        quantise(LAST + 1, n, n)
+        product_out(LAST - 1, 1, bank_name="t1_bank", copy=nc.vector.tensor_copy)
+        product_out(LAST, 0, n, n)
+        product_out(LAST, 1, n, n, copy=nc.vector.tensor_copy)

@@ -22,15 +22,15 @@ HALF = 512
 BLOCKS = HALF // P
 UNITS = NB * CO // HALF
 LAST = UNITS - 1
-W_COLS = BLOCKS * CV
+ROWS2 = 2 * CV
+W_COLS = 2 * ROWS2
 
-PAIR = 2 * CV
-OVERLAP = 16
-SHARE = slice(W_COLS - 448, W_COLS)
-SHARE_COLS = SHARE.stop - SHARE.start
+SHARE = 384
+OVERLAP = 2
 FIRST_SHARED = 2
 T1_LEAD = 3
 TURN_STEPS = 3
+WARM_UPS = 4
 
 
 def tile_cptensorproduct_pa_t_w4_kernel(tc, x1, A, t2, w_bytes, w_scale, C_words, C_scales, out):
@@ -43,10 +43,10 @@ def tile_cptensorproduct_pa_t_w4_kernel(tc, x1, A, t2, w_bytes, w_scale, C_words
         ctx.enter_context(tc.manual_schedule())
 
         x1_raw, t2_raw, w_raw = {}, {}, {}
-        w_share, w_bf = {}, {}
-        t2_turned, t2_codes, t2_scales = {}, {}, {}
-        t1_sb, joint, codes, scales = {}, {}, {}, {}
-        current = {}
+        w_wide, w_scaled, w_grouped, w_codes, w_scales = {}, {}, {}, {}, {}
+        t2_grouped, t2_codes, t2_scales = {}, {}, {}
+        t1_sb, h_grouped, h_codes, h_scales = {}, {}, {}, {}
+        turning = {}
 
         def load_w(i):
             b, half = divmod(i, 2)
@@ -65,71 +65,72 @@ def tile_cptensorproduct_pa_t_w4_kernel(tc, x1, A, t2, w_bytes, w_scale, C_words
         def scale_w(i, first, count):
             if i > LAST:
                 return
-            if i not in w_bf:
-                w_bf[i] = work.tile([P, W_COLS], BF16, name="w_scaled", align_bytes=64)
+            if i not in w_scaled:
+                w_scaled[i] = work.tile([P, W_COLS], BF16, name="w_bf16", align_bytes=64)
             cols = slice(first, first + count)
-            scales = scale_rows[:, first % CV : first % CV + count]
-            nc.vector.tensor_tensor(out=w_bf[i][:, cols], in0=w_raw[i][:, cols].bitcast(FP8), in1=scales, op=MULT)
+            factors = scale_rows[:, first % CV : first % CV + count]
+            nc.vector.tensor_tensor(out=w_scaled[i][:, cols], in0=w_raw[i][:, cols].bitcast(FP8), in1=factors, op=MULT)
 
         def widen_share(i):
             if i > LAST:
                 return
-            w_share[i] = work.tile([P, SHARE_COLS], BF16, name="w_widened")
-            nc.scalar.copy(out=w_share[i][:], in_=w_raw[i][:, SHARE].bitcast(FP8))
+            w_wide[i] = work.tile([P, SHARE], BF16, name="w_share")
+            nc.scalar.copy(out=w_wide[i][:], in_=w_raw[i][:, W_COLS - SHARE :].bitcast(FP8))
 
         def scale_share(i):
             if i > LAST:
                 return
-            scales = scale_rows[:, SHARE.start % CV : SHARE.start % CV + SHARE_COLS]
-            nc.gpsimd.tensor_tensor(out=w_bf[i][:, SHARE], in0=w_share[i][:], in1=scales, op=MULT)
+            factors = scale_rows[:, CV - SHARE : CV]
+            nc.gpsimd.tensor_tensor(out=w_scaled[i][:, W_COLS - SHARE :], in0=w_wide[i][:], in1=factors, op=MULT)
 
-        def turns(kind, index, pair):
-            return [(kind, index, pair, n) for n in range(4)]
+        def turns(kind, index, half):
+            return [(kind, index, half, n) for n in range(4)]
 
         def turn(step):
-            kind, index, pair, n = step
+            kind, index, half, n = step
             if index >= (UNITS if kind == "w" else NB):
                 return
+            raw, grouped = (w_scaled, w_grouped) if kind == "w" else (t2_raw, t2_grouped)
             if n == 0:
-                current["bank"] = psum.tile([P, 2, 2, P], F32, name="turn_bank")
-            bank = current["bank"]
-            if kind == "t2" and index not in t2_turned:
-                t2_turned[index] = work.tile([P, PACK * R], BF16, name="t2_grouped", align_bytes=64)
-            turned = joint_tile(index - 1)[:, 1, :] if kind == "w" else t2_turned[index][:]
-            words = (w_bf if kind == "w" else t2_raw)[index][:].bitcast(F32)
+                turning["bank"] = psum.tile([P, 2, 2, P], F32, name="turn_bank")
+            bank = turning["bank"]
+            if index not in grouped:
+                grouped[index] = work.tile([P, PACK * HALF], BF16, name=kind + "_by_column", align_bytes=64)
+            words = raw[index][:].bitcast(F32)
             j, u = divmod(n, 2)
-            first = (2 * pair + j) * CV // 2
+            first = (2 * half + j) * CV // 2
             nc.tensor.transpose(bank[:, j, u, :], words[:, first + u : first + CV // 2 : 2], ident[:])
             if n == 3:
-                group = turned.bitcast(F32)[:, 4 * P * pair : 4 * P * (pair + 1)]
-                nc.scalar.copy(out=group.rearrange("p (j r u) -> p j r u", j=2, u=2), in_=bank[:].rearrange("p j u r -> p j r u"))
+                target = grouped[index][:].bitcast(F32)[:, 4 * P * half : 4 * P * (half + 1)]
+                target = target.rearrange("p (j r u) -> p j r u", j=2, u=2)
+                nc.scalar.copy(out=target, in_=bank[:].rearrange("p j u r -> p j r u"))
 
-        def joint_tile(i):
-            if i not in joint:
-                joint[i] = work.tile([P, 2, PACK * HALF], BF16, name="h_and_w_grouped", align_bytes=64)
-            return joint[i]
+        def quantise_w(i):
+            if i > LAST:
+                return
+            w_codes[i] = work.tile([P, HALF], U32, name="w_code", align_bytes=64)
+            w_scales[i] = work.tile([P, HALF], U8, name="w_code_scale", align_bytes=64)
+            nc.vector.quantize_mx(out=w_codes[i][:].bitcast(FP8X4), scales=w_scales[i][:], in_=w_grouped[i][:])
 
-        def joint_codes(i):
-            if i not in codes:
-                codes[i] = work.tile([P, 2, HALF], U32, name="h_and_w_code", align_bytes=64)
-                scales[i] = work.tile([P, 2, HALF], U8, name="h_and_w_code_scale", align_bytes=64)
-            return codes[i][:].rearrange("p x n -> p (x n)"), scales[i][:].rearrange("p x n -> p (x n)")
-
-        def quantise(i, first, count):
-            code, scale = joint_codes(i)
-            n = slice(first, first + count)
-            wide = joint_tile(i)[:].rearrange("p x n -> p (x n)")[:, PACK * first : PACK * (first + count)]
-            nc.vector.quantize_mx(out=code[:, n].bitcast(FP8X4), scales=scale[:, n], in_=wide)
-
-        def quantise_t2(b, pair):
+        def quantise_t2(b, half):
             if b >= NB:
                 return
-            if pair == 0:
+            if half == 0:
                 t2_codes[b] = work.tile([P, R], U32, name="t2_code", align_bytes=64)
                 t2_scales[b] = work.tile([P, R], U8, name="t2_code_scale", align_bytes=64)
-            m = slice(2 * P * pair, 2 * P * (pair + 1))
-            wide = t2_turned[b][:, PACK * m.start : PACK * m.stop]
-            nc.vector.quantize_mx(out=t2_codes[b][:, m].bitcast(FP8X4), scales=t2_scales[b][:, m], in_=wide)
+            m = slice(R // 2 * half, R // 2 * (half + 1))
+            columns = t2_grouped[b][:, PACK * m.start : PACK * m.stop]
+            nc.vector.quantize_mx(out=t2_codes[b][:, m].bitcast(FP8X4), scales=t2_scales[b][:, m], in_=columns)
+
+        def quantise_h(i, first, count):
+            if i < 0:
+                return
+            if first == 0:
+                h_codes[i] = work.tile([P, HALF], U32, name="h_code", align_bytes=64)
+                h_scales[i] = work.tile([P, HALF], U8, name="h_code_scale", align_bytes=64)
+            n = slice(first, first + count)
+            columns = h_grouped[i][:, PACK * first : PACK * (first + count)]
+            nc.vector.quantize_mx(out=h_codes[i][:, n].bitcast(FP8X4), scales=h_scales[i][:, n], in_=columns)
 
         def product_t1(s, steps):
             if s < UNITS * BLOCKS:
@@ -143,9 +144,6 @@ def tile_cptensorproduct_pa_t_w4_kernel(tc, x1, A, t2, w_bytes, w_scale, C_words
                         nc.tensor.matmul(bank[:, t, :], lhsT=a_perm[:, k, t, :], rhs=rhs, start=(k == 0), stop=(k == 1))
                 t1_sb[s] = work.tile([P, P, PACK], F32, name="t1_copy", bufs=T1_LEAD + 4)
                 nc.scalar.copy(out=t1_sb[s][:], in_=bank[:].rearrange("p t o -> p o t"))
-            else:
-                for step in steps:
-                    turn(step)
 
         def product_t3(s):
             i, j = divmod(s, BLOCKS)
@@ -158,8 +156,8 @@ def tile_cptensorproduct_pa_t_w4_kernel(tc, x1, A, t2, w_bytes, w_scale, C_words
                     out=bank[:, t, :],
                     lhsT=t2_codes[b][:, m].bitcast(FP8X4),
                     lhsT_scale=t2_scales[b][:, m],
-                    rhs=codes[i - 1][:, 1, n].bitcast(FP8X4),
-                    rhs_scale=scales[i - 1][:, 1, n],
+                    rhs=w_codes[i][:, n].bitcast(FP8X4),
+                    rhs_scale=w_scales[i][:, n],
                     start=True,
                     stop=True,
                 )
@@ -167,7 +165,9 @@ def tile_cptensorproduct_pa_t_w4_kernel(tc, x1, A, t2, w_bytes, w_scale, C_words
 
         def multiply_h(s, bank):
             i, j = divmod(s, BLOCKS)
-            h = joint_tile(i + 1)[:, 0, PACK * P * j : PACK * P * (j + 1)].rearrange("p (o t) -> p o t", t=PACK)
+            if j == 0:
+                h_grouped[i] = work.tile([P, PACK * HALF], BF16, name="h_by_column", align_bytes=64)
+            h = h_grouped[i][:, PACK * P * j : PACK * P * (j + 1)].rearrange("p (o t) -> p o t", t=PACK)
             nc.vector.tensor_tensor(out=h, in0=bank[:].rearrange("p t o -> p o t"), in1=t1_sb[s][:], op=MULT)
 
         def product_out(i, m, first=0, count=HALF, bank_name="out_bank", copy=nc.scalar.copy):
@@ -180,8 +180,8 @@ def tile_cptensorproduct_pa_t_w4_kernel(tc, x1, A, t2, w_bytes, w_scale, C_words
                 out=bank[:, :count],
                 lhsT=c_words[:, 2 * P * m : 2 * P * (m + 1)].bitcast(FP4X4),
                 lhsT_scale=c_scales[:, P * m : P * (m + 1)],
-                rhs=codes[i + 1][:, 0, n].bitcast(FP8X4),
-                rhs_scale=scales[i + 1][:, 0, n],
+                rhs=h_codes[i][:, n].bitcast(FP8X4),
+                rhs_scale=h_scales[i][:, n],
                 start=True,
                 stop=True,
             )
@@ -190,11 +190,10 @@ def tile_cptensorproduct_pa_t_w4_kernel(tc, x1, A, t2, w_bytes, w_scale, C_words
             col = half * HALF + first
             nc.sync.dma_start(out=out[b, P * m : P * (m + 1), col : col + count], in_=result[:, :count])
 
-        scale_row = const.tile([P, CV], F32)
-        nc.vector.memset(scale_row[:], 0.0)
-        nc.scalar.dma_start(out=scale_row[0:1, :], in_=w_scale[0])
-        ones = const.tile([P, P], F32)
-        nc.vector.memset(ones[:], 1.0)
+        scale_cols = const.tile([P, PACK], F32)
+        nc.scalar.dma_start(out=scale_cols[:], in_=w_scale.rearrange("a b (p t) -> p (a b t)", t=PACK))
+        zeros = const.tile([P, HALF], BF16)
+        nc.vector.memset(zeros[:], 0.0)
         ident = const.tile([P, P], F32)
         make_identity(nc, ident[:])
         c_scales = const.tile([P, D], U8, align_bytes=64)
@@ -221,68 +220,70 @@ def tile_cptensorproduct_pa_t_w4_kernel(tc, x1, A, t2, w_bytes, w_scale, C_words
             load_x1(b)
             load_w(2 * b + 1)
 
-        bank = psum.tile([P, CV], F32, name="out_bank")
-        nc.tensor.matmul(bank[:], lhsT=ones[:], rhs=scale_row[:], start=True, stop=True)
+        warm_bank = psum.tile([P, HALF], F32, name="out_bank")
+        for repeat in range(WARM_UPS):
+            nc.tensor.matmul(warm_bank[:], lhsT=zeros[:, :P], rhs=zeros[:], start=True, stop=True)
+        row_bank = psum.tile([P, PACK, P], F32, name="out_bank")
+        for t in range(PACK):
+            column = scale_cols[:, t : t + 1].to_broadcast([P, P])
+            nc.tensor.matmul(row_bank[:, t, :], lhsT=column, rhs=ident[:], start=True, stop=True)
         scale_rows = const.tile([P, 2 * CV], F32)
-        nc.scalar.copy(out=scale_rows[:, :CV], in_=bank[:])
+        nc.scalar.copy(out=scale_rows[:, :CV].rearrange("p (q t) -> p q t", t=PACK), in_=row_bank[:].rearrange("p t q -> p q t"))
+
         for step in turns("t2", 0, 0) + turns("t2", 0, 1):
             turn(step)
         a_perm = const.tile([P, 2, PACK, P], BF16)
         nc.vector.tensor_copy(out=a_perm[:], in_=a_raw[:].rearrange("p k (m t) -> p k t m", t=PACK))
-        for s in range(2):
-            product_t1(s, [])
-        nc.scalar.copy(out=scale_rows[:, CV:], in_=bank[:])
+        product_t1(0, [])
+        product_t1(1, [])
+        nc.scalar.copy(out=scale_rows[:, CV:], in_=scale_rows[:, :CV])
         for j in range(BLOCKS):
             scale_w(0, CV * j, CV)
         for step in turns("w", 0, 0) + turns("w", 0, 1):
             turn(step)
-        for s in range(2, T1_LEAD):
-            product_t1(s, [])
+        product_t1(2, [])
         widen_share(FIRST_SHARED)
         quantise_t2(0, 0)
         quantise_t2(0, 1)
-        scale_w(1, 0, 2 * CV)
+        scale_w(1, 0, ROWS2)
         for step in turns("t2", 1, 0) + turns("w", 1, 0):
             turn(step)
-        quantise(-1, HALF, HALF)
+        quantise_w(0)
+        scale_w(1, ROWS2, ROWS2)
         quantise_t2(1, 0)
-        scale_w(1, 2 * CV, 2 * CV)
-        scale_w(2, PAIR, SHARE.start + OVERLAP - PAIR)
-        scale_share(2)
+        scale_w(FIRST_SHARED, ROWS2, ROWS2 - SHARE + OVERLAP)
+        scale_share(FIRST_SHARED)
 
         for i in range(UNITS):
             b, half = divmod(i, 2)
-            first_turns = turns("w", i + 1, 1) if i < LAST - 1 else []
-            middle_turns = turns("t2", b + 1 + half, 1 - half) if i < LAST - 2 else turns("w", i + 2, 1)
-            steps = first_turns + middle_turns + turns("w", i + 2, 0)
+            steps = turns("w", i + 1, 1) if i < LAST - 1 else []
+            steps += turns("t2", b + 1 + half, 1 - half) if i < LAST - 2 else turns("w", i + 2, 1)
+            steps += turns("w", i + 2, 0)
             for k in range(2):
-                pair = (BLOCKS * i + 2 * k, BLOCKS * i + 2 * k + 1)
-                banks = [product_t3(s) for s in pair]
+                blocks = (BLOCKS * i + 2 * k, BLOCKS * i + 2 * k + 1)
+                t3_banks = [product_t3(s) for s in blocks]
                 product_out(i - 2, k)
-                for s in pair:
+                for s in blocks:
                     first = TURN_STEPS * (s % BLOCKS)
                     product_t1(s + T1_LEAD, steps[first : first + TURN_STEPS])
-                for s, bank in zip(pair, banks):
+                for s, bank in zip(blocks, t3_banks):
                     multiply_h(s, bank)
                 if k == 0:
                     widen_share(i + 3)
-                    scale_w(i + 2, 0, PAIR)
-                    if i > 0:
-                        quantise(i, 0, HALF)
-                    if i < LAST:
-                        quantise(i, HALF, HALF)
-                    else:
-                        quantise(LAST + 1, 0, HALF // 2)
+                    scale_w(i + 2, 0, ROWS2)
+                    quantise_h(i - 1, 0, HALF)
+                    quantise_w(i + 1)
                 else:
-                    scale_w(i + 3, PAIR, SHARE.start + OVERLAP - PAIR)
+                    scale_w(i + 3, ROWS2, ROWS2 - SHARE + OVERLAP)
                     quantise_t2(b + 1 + half, 1 - half)
                     scale_share(i + 3)
+                if i == LAST:
+                    quantise_h(LAST, HALF // 2 * k, HALF // 2)
 
         n = HALF // 2
         product_out(LAST - 1, 0, bank_name="t1_bank")
-        for m in range(2):
-            product_out(LAST, m, 0, n, bank_name="t3_bank")
-        quantise(LAST + 1, n, n)
+        product_out(LAST, 0, 0, n, bank_name="t3_bank")
+        product_out(LAST, 1, 0, n, bank_name="t3_bank")
         product_out(LAST - 1, 1, bank_name="t1_bank", copy=nc.vector.tensor_copy)
         product_out(LAST, 0, n, n)
         product_out(LAST, 1, n, n, copy=nc.vector.tensor_copy)

from contextlib import ExitStack

import concourse.mybir as mybir
from concourse.masks import make_identity

NB, D, CO, CV, R = 8, 256, 1024, 512, 512
FLOPS = 2 * NB * (R * D * CO + R * CV * CO + D * R * CO)

F32 = mybir.dt.float32
BF16 = mybir.dt.bfloat16
I32 = mybir.dt.int32
U32 = mybir.dt.uint32
U8 = mybir.dt.uint8
FP8 = mybir.dt.float8_e4m3fn
FP8X4 = mybir.dt.float8_e4m3fn_x4
FP4X4 = mybir.dt.float4_e2m1fn_x4
MULT = mybir.AluOpType.mult

P = 128
PACK = 4
HALF = 512
BLOCKS = HALF // P
UNITS = NB * CO // HALF
LAST = UNITS - 1
ROWS2 = 2 * CV
W_COLS = 2 * ROWS2

SHARE = 384
OVERLAP = 2
FIRST_SHARED = 2
T1_LEAD = 3
TURN_STEPS = 3
WARM_UPS = 4


def tile_cptensorproduct_pa_t_w4_kernel(tc, x1, A, t2, w_bytes, w_scale, C_words, C_scales, out):
    nc = tc.nc
    with ExitStack() as ctx:
        const = ctx.enter_context(tc.tile_pool(name="const", bufs=1))
        loads = ctx.enter_context(tc.tile_pool(name="loads", bufs=NB))
        work = ctx.enter_context(tc.tile_pool(name="work", bufs=3))
        psum = ctx.enter_context(tc.psum_pool(name="psum", bufs=2))
        ctx.enter_context(tc.manual_schedule())

        x1_raw, t2_raw, w_raw = {}, {}, {}
        w_wide, w_scaled, w_grouped, w_codes, w_scales = {}, {}, {}, {}, {}
        t2_grouped, t2_codes, t2_scales = {}, {}, {}
        t1_sb, h_grouped, h_codes, h_scales = {}, {}, {}, {}
        turning = {}

        def load_w(i):
            b, half = divmod(i, 2)
            w_raw[i] = loads.tile([P, W_COLS], U8, name="w_raw_bytes", bufs=UNITS)
            rows = w_bytes[b, half * HALF : (half + 1) * HALF, :].rearrange("(j p) c -> p j c", p=P)
            nc.sync.dma_start(out=w_raw[i][:].rearrange("p (j c) -> p j c", j=BLOCKS), in_=rows)

        def load_t2(b):
            t2_raw[b] = loads.tile([P, PACK * CV], BF16, name="t2_rows")
            nc.sync.dma_start(out=t2_raw[b][:], in_=t2[b].rearrange("(m t) c -> m (t c)", t=PACK))

        def load_x1(b):
            x1_raw[b] = loads.tile([P, 2, CO], BF16, name="x1_rows")
            nc.sync.dma_start(out=x1_raw[b][:], in_=x1[b].rearrange("(p k) o -> p k o", k=2))

        def scale_w(i, first, count):
            if i > LAST:
                return
            if i not in w_scaled:
                w_scaled[i] = work.tile([P, W_COLS], BF16, name="w_bf16", align_bytes=64)
            cols = slice(first, first + count)
            factors = scale_rows[:, first % CV : first % CV + count]
            nc.vector.tensor_tensor(out=w_scaled[i][:, cols], in0=w_raw[i][:, cols].bitcast(FP8), in1=factors, op=MULT)

        def widen_share(i):
            if i > LAST:
                return
            w_wide[i] = work.tile([P, SHARE], BF16, name="w_share")
            nc.scalar.copy(out=w_wide[i][:], in_=w_raw[i][:, W_COLS - SHARE :].bitcast(FP8))

        def scale_share(i):
            if i > LAST:
                return
            factors = scale_rows[:, CV - SHARE : CV]
            nc.gpsimd.tensor_tensor(out=w_scaled[i][:, W_COLS - SHARE :], in0=w_wide[i][:], in1=factors, op=MULT)

        def turns(kind, index, half):
            return [(kind, index, half, n) for n in range(4)]

        def turn(step):
            kind, index, half, n = step
            if index >= (UNITS if kind == "w" else NB):
                return
            raw, grouped = (w_scaled, w_grouped) if kind == "w" else (t2_raw, t2_grouped)
            if n == 0:
                turning["bank"] = psum.tile([P, 2, 2, P], F32, name="turn_bank")
            bank = turning["bank"]
            if index not in grouped:
                grouped[index] = work.tile([P, PACK * HALF], BF16, name=kind + "_by_column", align_bytes=64)
            words = raw[index][:].bitcast(F32)
            j, u = divmod(n, 2)
            first = (2 * half + j) * CV // 2
            nc.tensor.transpose(bank[:, j, u, :], words[:, first + u : first + CV // 2 : 2], ident[:])
            if n == 3:
                target = grouped[index][:].bitcast(F32)[:, 4 * P * half : 4 * P * (half + 1)]
                target = target.rearrange("p (j r u) -> p j r u", j=2, u=2)
                nc.scalar.copy(out=target, in_=bank[:].rearrange("p j u r -> p j r u"))

        def quantise_w(i):
            if i > LAST:
                return
            w_codes[i] = work.tile([P, HALF], U32, name="w_code", align_bytes=64)
            w_scales[i] = work.tile([P, HALF], U8, name="w_code_scale", align_bytes=64)
            nc.vector.quantize_mx(out=w_codes[i][:].bitcast(FP8X4), scales=w_scales[i][:], in_=w_grouped[i][:])

        def quantise_t2(b, half):
            if b >= NB:
                return
            if half == 0:
                t2_codes[b] = work.tile([P, R], U32, name="t2_code", align_bytes=64)
                t2_scales[b] = work.tile([P, R], U8, name="t2_code_scale", align_bytes=64)
            m = slice(R // 2 * half, R // 2 * (half + 1))
            columns = t2_grouped[b][:, PACK * m.start : PACK * m.stop]
            nc.vector.quantize_mx(out=t2_codes[b][:, m].bitcast(FP8X4), scales=t2_scales[b][:, m], in_=columns)

        def quantise_h(i, first, count):
            if i < 0:
                return
            if first == 0:
                h_codes[i] = work.tile([P, HALF], U32, name="h_code", align_bytes=64)
                h_scales[i] = work.tile([P, HALF], U8, name="h_code_scale", align_bytes=64)
            n = slice(first, first + count)
            columns = h_grouped[i][:, PACK * first : PACK * (first + count)]
            nc.vector.quantize_mx(out=h_codes[i][:, n].bitcast(FP8X4), scales=h_scales[i][:, n], in_=columns)

        def product_t1(s, steps):
            if s < UNITS * BLOCKS:
                b, block = divmod(s, CO // P)
                bank = psum.tile([P, PACK, P], F32, name="t1_bank")
                for t in range(PACK):
                    if 0 < t <= len(steps):
                        turn(steps[t - 1])
                    for k in range(2):
                        rhs = x1_raw[b][:, k, P * block : P * (block + 1)]
                        nc.tensor.matmul(bank[:, t, :], lhsT=a_perm[:, k, t, :], rhs=rhs, start=(k == 0), stop=(k == 1))
                t1_sb[s] = work.tile([P, P, PACK], F32, name="t1_copy", bufs=T1_LEAD + 4)
                nc.scalar.copy(out=t1_sb[s][:], in_=bank[:].rearrange("p t o -> p o t"))

        def product_t3(s):
            i, j = divmod(s, BLOCKS)
            b = i // 2
            bank = psum.tile([P, PACK, P], F32, name="t3_bank")
            n = slice(P * j, P * (j + 1))
            for t in range(PACK):
                m = slice(P * t, P * (t + 1))
                nc.tensor.matmul_mx(
                    out=bank[:, t, :],
                    lhsT=t2_codes[b][:, m].bitcast(FP8X4),
                    lhsT_scale=t2_scales[b][:, m],
                    rhs=w_codes[i][:, n].bitcast(FP8X4),
                    rhs_scale=w_scales[i][:, n],
                    start=True,
                    stop=True,
                )
            return bank

        def multiply_h(s, bank):
            i, j = divmod(s, BLOCKS)
            if j == 0:
                h_grouped[i] = work.tile([P, PACK * HALF], BF16, name="h_by_column", align_bytes=64)
            h = h_grouped[i][:, PACK * P * j : PACK * P * (j + 1)].rearrange("p (o t) -> p o t", t=PACK)
            nc.vector.tensor_tensor(out=h, in0=bank[:].rearrange("p t o -> p o t"), in1=t1_sb[s][:], op=MULT)

        def product_out(i, m, first=0, count=HALF, bank_name="out_bank", copy=nc.scalar.copy):
            if i < 0:
                return
            b, half = divmod(i, 2)
            n = slice(first, first + count)
            bank = psum.tile([P, HALF], F32, name=bank_name)
            nc.tensor.matmul_mx(
                out=bank[:, :count],
                lhsT=c_words[:, 2 * P * m : 2 * P * (m + 1)].bitcast(FP4X4),
                lhsT_scale=c_scales[:, P * m : P * (m + 1)],
                rhs=h_codes[i][:, n].bitcast(FP8X4),
                rhs_scale=h_scales[i][:, n],
                start=True,
                stop=True,
            )
            result = work.tile([P, HALF], F32, name="out_copy", bufs=8)
            copy(out=result[:, :count], in_=bank[:, :count])
            col = half * HALF + first
            nc.sync.dma_start(out=out[b, P * m : P * (m + 1), col : col + count], in_=result[:, :count])

        scale_cols = const.tile([P, PACK], F32)
        nc.scalar.dma_start(out=scale_cols[:], in_=w_scale.rearrange("a b (p t) -> p (a b t)", t=PACK))
        zeros = const.tile([P, HALF], BF16)
        nc.vector.memset(zeros[:], 0.0)
        ident = const.tile([P, P], F32)
        make_identity(nc, ident[:])
        c_scales = const.tile([P, D], U8, align_bytes=64)
        nc.vector.memset(c_scales[:].bitcast(I32), 0)

        load_w(0)
        a_raw = const.tile([P, 2, R], BF16)
        nc.sync.dma_start(out=a_raw[:], in_=A.rearrange("(p k) r -> p k r", k=2))
        load_t2(0)
        load_x1(0)
        load_w(1)
        load_w(2)
        load_t2(1)
        load_x1(1)
        load_w(3)
        c_words = const.tile([P, 2 * D], U8, align_bytes=64)
        nc.sync.dma_start(out=c_words[:], in_=C_words[0])
        for q in range(4):
            rows = C_scales[0, 4 * q : 4 * q + 4, :].bitcast(I32)
            nc.sync.dma_start(out=c_scales[32 * q : 32 * q + 4, :].bitcast(I32), in_=rows)
        for b in range(2, NB):
            load_w(2 * b)
            load_t2(b)
            load_x1(b)
            load_w(2 * b + 1)

        warm_bank = psum.tile([P, HALF], F32, name="out_bank")
        for repeat in range(WARM_UPS):
            nc.tensor.matmul(warm_bank[:], lhsT=zeros[:, :P], rhs=zeros[:], start=True, stop=True)
        row_bank = psum.tile([P, PACK, P], F32, name="out_bank")
        for t in range(PACK):
            column = scale_cols[:, t : t + 1].to_broadcast([P, P])
            nc.tensor.matmul(row_bank[:, t, :], lhsT=column, rhs=ident[:], start=True, stop=True)
        scale_rows = const.tile([P, 2 * CV], F32)
        nc.scalar.copy(out=scale_rows[:, :CV].rearrange("p (q t) -> p q t", t=PACK), in_=row_bank[:].rearrange("p t q -> p q t"))

        for step in turns("t2", 0, 0) + turns("t2", 0, 1):
            turn(step)
        a_perm = const.tile([P, 2, PACK, P], BF16)
        nc.vector.tensor_copy(out=a_perm[:], in_=a_raw[:].rearrange("p k (m t) -> p k t m", t=PACK))
        product_t1(0, [])
        product_t1(1, [])
        nc.scalar.copy(out=scale_rows[:, CV:], in_=scale_rows[:, :CV])
        for j in range(BLOCKS):
            scale_w(0, CV * j, CV)
        for step in turns("w", 0, 0) + turns("w", 0, 1):
            turn(step)
        product_t1(2, [])
        widen_share(FIRST_SHARED)
        quantise_t2(0, 0)
        quantise_t2(0, 1)
        scale_w(1, 0, ROWS2)
        for step in turns("t2", 1, 0) + turns("w", 1, 0):
            turn(step)
        quantise_w(0)
        scale_w(1, ROWS2, ROWS2)
        quantise_t2(1, 0)
        scale_w(FIRST_SHARED, ROWS2, ROWS2 - SHARE + OVERLAP)
        scale_share(FIRST_SHARED)

        for i in range(UNITS):
            b, half = divmod(i, 2)
            steps = turns("w", i + 1, 1) if i < LAST - 1 else []
            steps += turns("t2", b + 1 + half, 1 - half) if i < LAST - 2 else turns("w", i + 2, 1)
            steps += turns("w", i + 2, 0)
            for k in range(2):
                blocks = (BLOCKS * i + 2 * k, BLOCKS * i + 2 * k + 1)
                t3_banks = [product_t3(s) for s in blocks]
                product_out(i - 2, k)
                for s in blocks:
                    first = TURN_STEPS * (s % BLOCKS)
                    product_t1(s + T1_LEAD, steps[first : first + TURN_STEPS])
                for s, bank in zip(blocks, t3_banks):
                    multiply_h(s, bank)
                if k == 0:
                    widen_share(i + 3)
                    scale_w(i + 2, 0, ROWS2)
                    quantise_h(i - 1, 0, HALF)
                    quantise_w(i + 1)
                else:
                    scale_w(i + 3, ROWS2, ROWS2 - SHARE + OVERLAP)
                    quantise_t2(b + 1 + half, 1 - half)
                    scale_share(i + 3)
                if i == LAST:
                    quantise_h(LAST, HALF // 2 * k, HALF // 2)

        n = HALF // 2
        product_out(LAST - 1, 0, bank_name="t1_bank")
        product_out(LAST, 0, 0, n, bank_name="t3_bank")
        product_out(LAST, 1, 0, n, bank_name="t3_bank")
        product_out(LAST - 1, 1, bank_name="t1_bank", copy=nc.vector.tensor_copy)
        product_out(LAST, 0, n, n)
        product_out(LAST, 1, n, n, copy=nc.vector.tensor_copy)
